import numpy as np
import ml_dtypes


def mxq(x, axis, fmt="e4m3"):
    dtype, down = {"e4m3": (ml_dtypes.float8_e4m3fn, 7), "e5m2": (ml_dtypes.float8_e5m2, 14)}[fmt]
    v = np.moveaxis(np.asarray(x, np.float32).astype(ml_dtypes.bfloat16).astype(np.float64), axis, -1)
    blocks = v.reshape(v.shape[:-1] + (-1, 32))
    amax = np.abs(blocks).max(-1, keepdims=True)
    byte = np.maximum(np.where(amax > 0, np.frexp(amax)[1] - 1 + 127, 0) - down, 1)
    scale = np.exp2(byte - 127.0)
    codes = (blocks / scale).astype(np.float32).astype(dtype).astype(np.float64)
    return np.moveaxis((codes * scale).reshape(v.shape), -1, axis)


WIDE = False


def mx_kscale(k):
    if not WIDE:
        return np.ones(k)
    levels = np.array([10, -10, 5, -5, 0])
    if k % 512:
        return np.exp2(np.random.permutation(np.resize(levels, k // 32))).repeat(32)
    a = np.empty((k // 512, 16))
    for p in range(k // 512):
        a[p, :8] = np.random.permutation(np.resize(levels, 8))
        for g in range(8):
            far = levels[np.abs(levels - a[p, g]) >= 10]
            a[p, g + 8] = far[np.random.randint(len(far))]
    return np.exp2(a.ravel()).repeat(32)


BF16 = ml_dtypes.bfloat16


def bf(x):
    return np.asarray(x, np.float32).astype(BF16)


def f64(x):
    return np.asarray(x).astype(np.float64)


B, H, W, C, NS = 2, 2, 1024, 128, 2
WIN = W // NS
SHIFT = WIN // 2


def setup_inputs():
    s = mx_kscale(WIN)
    sv = np.roll(np.tile(s.max() / s, NS), SHIFT)
    return {"q": bf(np.random.standard_normal((B, H * W, C))),
            "k": bf(np.random.standard_normal((B, H * W, C))),
            "v": bf((np.random.standard_normal((B, H, W, C)) * 2.0 * sv[None, None, :, None]).reshape(B, H * W, C)),
            "attn_mask": bf(np.random.standard_normal((NS, WIN, WIN)) + np.log(s)[None, None, :]),
            "h": H, "w": W, "num_splits": NS}


def reference(q, k, v, attn_mask, h, w, num_splits):
    b, hw, c = q.shape
    assert hw == h * w
    win = w // num_splits
    shift = win // 2
    scale = c ** 0.5

    def prep(x):
        x = f64(x).reshape(b * h, w, c)
        x = np.roll(x, -shift, axis=1)
        return x.reshape(b * h, num_splits, win, c)

    qs, ks, vs = prep(q), prep(k), prep(v)
    scores = qs @ ks.transpose(0, 1, 3, 2) / scale
    scores = scores + f64(attn_mask)[None]
    e = np.exp(scores - scores.max(-1, keepdims=True))
    out = (mxq(e, 3, "e4m3") @ mxq(vs, 2, "e4m3")) / e.sum(-1, keepdims=True)
    out = out.reshape(b, h, w, c)
    out = np.roll(out, shift, axis=2)
    return out.reshape(b, h * w, c)

@@ -1,0 +1,411 @@
+from contextlib import ExitStack
+
+import concourse.mybir as mybir
+from concourse.masks import make_identity
+
+BF16 = mybir.dt.bfloat16
+F32 = mybir.dt.float32
+U32 = mybir.dt.uint32
+U8 = mybir.dt.uint8
+FP8X4 = mybir.dt.float8_e4m3fn_x4
+ALU = mybir.AluOpType
+ACT = mybir.ActivationFunctionType
+
+P = 128
+C = 128
+ROWS = 4
+WIN = 512
+NWIN = 2
+UNITS = ROWS * NWIN
+PAIRS = 2 * UNITS
+FLOPS = 2 * UNITS * 2 * WIN * WIN * C
+
+
+def tile_single_head_split_window_attention_1d_kernel(
+    tc, q, k, v, attn_mask, h, w, num_splits, out
+):
+    nc = tc.nc
+    assert h == 2 and w == 1024 and num_splits == 2
+    scale = 1.0 / (C ** 0.5)
+
+    q_v = q.flatten_outer_dims().rearrange("(g p j) c -> p g j c", p=P, j=2)
+    k_v = k.flatten_outer_dims().rearrange("(t p) c -> p t c", p=P)
+    v_v = v.flatten_outer_dims().rearrange("(g p t) c -> g p t c", p=P // 2, t=4)
+    b_v = attn_mask.rearrange("n (h p j) k -> p n h j k", p=P, j=2)
+    o_v = out.flatten_outer_dims().rearrange("(g p j) c -> p g j c", p=P, j=2)
+
+    with ExitStack() as ctx:
+        const = ctx.enter_context(tc.tile_pool(name="const", bufs=1))
+        work = ctx.enter_context(tc.tile_pool(name="work", bufs=4))
+        stat = ctx.enter_context(tc.tile_pool(name="stat", bufs=8))
+        ps_t = ctx.enter_context(tc.psum_pool(name="ps_t", bufs=1))
+        ps_s = ctx.enter_context(tc.psum_pool(name="ps_s", bufs=4))
+        ps_e = ctx.enter_context(tc.psum_pool(name="ps_e", bufs=2))
+        ps_o = ctx.enter_context(tc.psum_pool(name="ps_o", bufs=1))
+        ctx.enter_context(tc.manual_schedule())
+
+        k_sb = [const.tile([P, 4, C], BF16, name="k_sb%d" % u) for u in range(UNITS)]
+        q_sb = [const.tile([P, 2, 2, C], BF16, name="q_sb%d" % u) for u in range(UNITS)]
+        v_sb = [const.tile([P, 4, C], BF16, name="v_sb%d" % u) for u in range(UNITS)]
+        b_sb = [
+            [const.tile([P, 2, WIN], BF16, name="b_sb%d%d" % (n, hh)) for hh in range(2)]
+            for n in range(NWIN)
+        ]
+
+        def load_tiles(dst, src, u):
+            r, n = u % ROWS, u // ROWS
+            if n == 0:
+                nc.sync.dma_start(out=dst[:], in_=src[:, 8 * r + 2 : 8 * r + 6, :])
+            else:
+                nc.sync.dma_start(out=dst[:, 0:2, :], in_=src[:, 8 * r + 6 : 8 * r + 8, :])
+                nc.sync.dma_start(out=dst[:, 2:4, :], in_=src[:, 8 * r : 8 * r + 2, :])
+
+        def load_q(u):
+            r, n = u % ROWS, u // ROWS
+            if n == 0:
+                nc.sync.dma_start(out=q_sb[u][:], in_=q_v[:, 4 * r + 1 : 4 * r + 3, :, :])
+            else:
+                nc.sync.dma_start(out=q_sb[u][:, 0], in_=q_v[:, 4 * r + 3, :, :])
+                nc.sync.dma_start(out=q_sb[u][:, 1], in_=q_v[:, 4 * r, :, :])
+
+        def load_v(u):
+            r, n = u % ROWS, u // ROWS
+            for hh in range(2):
+                nc.sync.dma_start(
+                    out=v_sb[u][64 * hh : 64 * hh + 64],
+                    in_=v_v[4 * r + (1 + 2 * n + hh) % 4],
+                )
+
+        def load_bias(n):
+            for hh in range(2):
+                nc.sync.dma_start(out=b_sb[n][hh][:], in_=b_v[:, n, hh])
+
+        for u in range(UNITS):
+            load_tiles(k_sb[u], k_v, u)
+            load_q(u)
+            if u == 0:
+                load_bias(0)
+            else:
+                load_v(u - 1)
+            if u == 1:
+                load_bias(1)
+        load_v(UNITS - 1)
+
+        ident = const.tile([P, P], BF16, name="ident")
+        make_identity(nc, ident[:])
+        ident_f = const.tile([P, P], F32, name="ident_f")
+        make_identity(nc, ident_f[:])
+        warm = const.tile([P, 1], F32, name="warm")
+        nc.vector.memset(warm[:], 0.0)
+        warm2 = const.tile([P, 1], F32, name="warm2")
+        nc.scalar.activation(out=warm2[:], in_=warm[:], func=ACT.Exp)
+
+        zeros = const.tile([P, WIN], BF16, name="zeros")
+        nc.vector.memset(zeros[:], 0.0)
+        for d in range(3):
+            z_ps = ps_s.tile([P, WIN], F32, name="z_ps", tag="s_ps")
+            nc.tensor.matmul(out=z_ps[:], lhsT=ident[:], rhs=zeros[:], start=True, stop=True)
+
+        bp = [const.tile([P, 4, 4, P], F32, name="bp%d" % n) for n in range(NWIN)]
+        v_codes = [const.tile([P, C], U32, name="v_codes%d" % u, align_bytes=64) for u in range(UNITS)]
+        v_scales = [const.tile([P, C], U8, name="v_scales%d" % u, align_bytes=64) for u in range(UNITS)]
+
+        live = {}
+
+        def bias_t(n, a0, na, spare):
+            if spare:
+                bT = ps_o.tile([P, na, 4, P], BF16, name="bT", tag="o_ps")
+            else:
+                bT = ps_e.tile([P, na, 4, P], BF16, name="bT", tag="eT")
+            for a in range(na):
+                for t in range(4):
+                    nc.tensor.transpose(
+                        out=bT[:, a, t, :],
+                        in_=b_sb[n][(a0 + a) // 2][:, (a0 + a) % 2, P * t : P * t + P],
+                        identity=ident[:],
+                    )
+            live["bT", n, a0] = bT
+
+        def bias_ev(n, a0, na, on_vector):
+            bT = live["bT", n, a0]
+            if on_vector:
+                nc.vector.tensor_scalar_mul(
+                    out=bp[n][:, a0 : a0 + na, :, :], in0=bT[:], scalar1=C ** 0.5
+                )
+            else:
+                nc.scalar.mul(out=bp[n][:, a0 : a0 + na, :, :], in_=bT[:], mul=C ** 0.5)
+
+        def tqk(u):
+            t_ps = ps_t.tile([P, 8, P], BF16, name="t_ps")
+            for t in range(4):
+                nc.tensor.transpose(out=t_ps[:, t, :], in_=k_sb[u][:, t, :], identity=ident[:])
+            for a in range(4):
+                nc.tensor.transpose(
+                    out=t_ps[:, 4 + a, :], in_=q_sb[u][:, a // 2, a % 2, :], identity=ident[:]
+                )
+            live["t_ps", u] = t_ps
+
+        def evqk(u):
+            qkT = work.tile([P, 8, P], BF16, name="qkT")
+            nc.vector.tensor_copy(out=qkT[:], in_=live["t_ps", u][:])
+            live["qkT", u] = qkT
+
+        def vprep(u):
+            gv = work.tile([P, C, 4], BF16, name="gv", align_bytes=64)
+            nc.gpsimd.tensor_scalar(
+                out=gv[:],
+                in0=v_sb[u][:].rearrange("p t c -> p c t"),
+                scalar1=1.0,
+                scalar2=0.0,
+                op0=ALU.mult,
+                op1=ALU.add,
+            )
+            live["gv", u] = gv
+
+        def vquant(u):
+            nc.vector.quantize_mx(
+                out=v_codes[u][:].bitcast(FP8X4),
+                scales=v_scales[u][:],
+                in_=live["gv", u][:].rearrange("p c t -> p (c t)"),
+            )
+
+        def qk(i):
+            u, a = i // 4, i % 4
+            qkT = live["qkT", u]
+            s_ps = ps_s.tile([P, WIN], F32, name="s_ps")
+            nc.tensor.matmul(
+                out=s_ps[:],
+                lhsT=qkT[:, 4 + a, :],
+                rhs=qkT[:, 0:4, :].rearrange("p t k -> p (t k)"),
+                start=True,
+                stop=False,
+            )
+            live["s_ps", i] = s_ps
+
+        def addbias(i):
+            u, a = i // 4, i % 4
+            for t in range(4):
+                nc.tensor.matmul(
+                    out=live["s_ps", i][:, P * t : P * t + P],
+                    lhsT=bp[u // ROWS][:, a, t, :],
+                    rhs=ident_f[:],
+                    is_transpose=True,
+                    start=False,
+                    stop=(t == 3),
+                )
+
+        def rowmax(i):
+            sp = work.tile([P, 4, P], F32, name="sp")
+            negmax = stat.tile([P, 1], F32, name="negmax")
+            nc.vector.tensor_scalar(
+                out=sp[:],
+                in0=live["s_ps", i][:].rearrange("q (p t) -> q t p", t=4),
+                scalar1=-scale,
+                scalar2=None,
+                op0=ALU.mult,
+                op1=ALU.min,
+                accum_out=negmax[:],
+            )
+            live["sp", i] = (sp, negmax)
+
+        def expo(i):
+            u, a = i // 4, i % 4
+            if a == 0:
+                live["rowsum", u] = stat.tile([P, 4], F32, name="rowsum")
+            if a % 2 == 0:
+                live["e", i // 2] = work.tile([P, 2, WIN], BF16, name="e_sb")
+            sp, negmax = live["sp", i]
+            nc.scalar.activation(
+                out=live["e", i // 2][:, a % 2, :],
+                in_=sp[:].rearrange("q t p -> q (t p)"),
+                func=ACT.Exp,
+                bias=negmax[:],
+                scale=-1.0,
+                accum_out=live["rowsum", u][:, a : a + 1],
+            )
+
+        def te(j):
+            eT = ps_e.tile([P, 2, 4, P], BF16, name="eT")
+            for a in range(2):
+                for t in range(4):
+                    nc.tensor.transpose(
+                        out=eT[:, a, t, :],
+                        in_=live["e", j][:, a, P * t : P * t + P],
+                        identity=ident[:],
+                    )
+            live["eT", j] = eT
+
+        def eve(j, on_vector):
+            g_sb = work.tile([P, 2, P, 4], BF16, name="g_sb", align_bytes=64)
+            if on_vector:
+                nc.vector.tensor_copy(
+                    out=g_sb[:], in_=live["eT", j][:].rearrange("p a t q -> p a q t")
+                )
+            else:
+                nc.scalar.copy(out=g_sb[:], in_=live["eT", j][:].rearrange("p a t q -> p a q t"))
+            live["g", j] = g_sb
+
+        def te_one(i):
+            eT1 = ps_s.tile([P, 4, P], BF16, name="eT1", tag="s_ps")
+            for t in range(4):
+                nc.tensor.transpose(
+                    out=eT1[:, t, :],
+                    in_=live["e", i // 2][:, i % 2, P * t : P * t + P],
+                    identity=ident[:],
+                )
+            live["eT1", i] = eT1
+
+        def eve_one(i, on_vector):
+            if i % 2 == 0:
+                live["g", i // 2] = work.tile([P, 2, P, 4], BF16, name="g_sb", align_bytes=64)
+            dst = live["g", i // 2][:, i % 2, :, :]
+            if on_vector:
+                nc.vector.tensor_copy(out=dst, in_=live["eT1", i][:].rearrange("p t q -> p q t"))
+            else:
+                nc.scalar.copy(out=dst, in_=live["eT1", i][:].rearrange("p t q -> p q t"))
+
+        def qnt(j):
+            u, b = j // 2, j % 2
+            if b == 0:
+                live["c", u] = (
+                    work.tile([P, 4 * P], U32, name="e_codes", align_bytes=64),
+                    work.tile([P, 4 * P], U8, name="e_scales", align_bytes=64),
+                )
+            e_codes, e_scales = live["c", u]
+            nc.vector.quantize_mx(
+                out=e_codes[:, 2 * P * b : 2 * P * b + 2 * P].bitcast(FP8X4),
+                scales=e_scales[:, 2 * P * b : 2 * P * b + 2 * P],
+                in_=live["g", j][:].rearrange("p a q t -> p (a q t)"),
+            )
+
+        def mxu(u, spare):
+            e_codes, e_scales = live["c", u]
+            if spare:
+                o_ps = ps_s.tile([P, 4, C], F32, name="o_ps", tag="s_ps")
+            else:
+                o_ps = ps_o.tile([P, 4, C], F32, name="o_ps")
+            for a in range(4):
+                nc.tensor.matmul_mx(
+                    out=o_ps[:, a, :],
+                    lhsT=e_codes[:, P * a : P * a + P].bitcast(FP8X4),
+                    lhsT_scale=e_scales[:, P * a : P * a + P],
+                    rhs=v_codes[u][:].bitcast(FP8X4),
+                    rhs_scale=v_scales[u][:],
+                    start=True,
+                    stop=True,
+                )
+            live["o", u] = o_ps
+
+        def recip(u):
+            rinv = stat.tile([P, 4], F32, name="rinv")
+            nc.vector.reciprocal(out=rinv[:], in_=live["rowsum", u][:])
+            live["rinv", u] = rinv
+
+        def outu(u, on_vector):
+            r, n = u % ROWS, u // ROWS
+            rinv = live["rinv", u]
+            o_sb = work.tile([P, 4, C], F32, name="o_sb")
+            if on_vector:
+                nc.vector.tensor_tensor(
+                    out=o_sb[:],
+                    in0=live["o", u][:],
+                    in1=rinv[:].unsqueeze(2).to_broadcast([P, 4, C]),
+                    op=ALU.mult,
+                )
+            else:
+                for a in range(4):
+                    nc.scalar.activation(
+                        out=o_sb[:, a, :],
+                        in_=live["o", u][:, a, :],
+                        func=ACT.Copy,
+                        scale=rinv[:, a : a + 1],
+                    )
+            for hh in range(2):
+                g = 4 * r + (1 + 2 * n + hh) % 4
+                nc.sync.dma_start(out=o_v[:, g, :, :], in_=o_sb[:, 2 * hh : 2 * hh + 2, :])
+
+        tqk(0)
+        evqk(0)
+        bias_t(0, 0, 1, False)
+        bias_t(0, 1, 1, False)
+        bias_ev(0, 0, 1, True)
+        bias_ev(0, 1, 1, False)
+
+        for s in range(PAIRS - 1):
+            m = s - 1
+            unit_out = (s - 6) // 2 if s % 2 == 0 else -1
+            if s in (3, 4):
+                bias_t(1, 2 * (s - 3), 2, True)
+            qk(2 * s)
+            qk(2 * s + 1)
+            addbias(2 * s)
+            addbias(2 * s + 1)
+            if unit_out >= 0:
+                mxu(unit_out, False)
+            if s == 0:
+                bias_t(0, 2, 2, True)
+            if s % 2 == 0 and s // 2 + 1 < UNITS:
+                tqk(s // 2 + 1)
+            if s >= 2:
+                te(s - 2)
+            if m >= 0:
+                rowmax(2 * m)
+                rowmax(2 * m + 1)
+            if m >= 0 and m % 2 == 0:
+                evqk(m // 2 + 1)
+            if m >= 3:
+                qnt(m - 3)
+            if m >= 0 and m % 2 == 0:
+                vquant(m // 2)
+            if unit_out >= 0:
+                recip(unit_out)
+                outu(unit_out, True)
+            if s in (3, 4):
+                bias_ev(1, 2 * (s - 3), 2, True)
+            if s == 0:
+                bias_ev(0, 2, 2, False)
+            if m >= 0:
+                expo(2 * m)
+                expo(2 * m + 1)
+            if m >= 1:
+                eve(m - 1, False)
+            if s % 2 == 0:
+                vprep(s // 2)
+
+        qk(30)
+        qk(31)
+        addbias(30)
+        addbias(31)
+        te(13)
+        rowmax(28)
+        rowmax(29)
+        qnt(11)
+        vquant(7)
+        expo(28)
+        expo(29)
+
+        mxu(5, False)
+        te(14)
+        rowmax(30)
+        rowmax(31)
+        expo(30)
+        expo(31)
+        te_one(30)
+        te_one(31)
+        eve(13, True)
+        qnt(12)
+        recip(5)
+        outu(5, True)
+        qnt(13)
+        eve_one(30, True)
+        eve(14, False)
+        eve_one(31, False)
+
+        mxu(6, False)
+        recip(6)
+        qnt(14)
+        qnt(15)
+        recip(7)
+        outu(6, False)
+        mxu(7, True)
+        outu(7, True)

@@ -195,11 +195,11 @@ def tile_single_head_split_window_attention_1d_kernel(
                 )
 
         def rowmax(i):
-            sp = work.tile([P, 4, P], F32, name="sp")
+            sp = work.tile([P, 2, P, 2], F32, name="sp")
             negmax = stat.tile([P, 1], F32, name="negmax")
             nc.vector.tensor_scalar(
                 out=sp[:],
-                in0=live["s_ps", i][:].rearrange("q (p t) -> q t p", t=4),
+                in0=live["s_ps", i][:].rearrange("q (p u e) -> q u p e", u=2, e=2),
                 scalar1=-scale,
                 scalar2=None,
                 op0=ALU.mult,
@@ -217,7 +217,7 @@ def tile_single_head_split_window_attention_1d_kernel(
             sp, negmax = live["sp", i]
             nc.scalar.activation(
                 out=live["e", i // 2][:, a % 2, :],
-                in_=sp[:].rearrange("q t p -> q (t p)"),
+                in_=sp[:].rearrange("q u p e -> q (u p e)"),
                 func=ACT.Exp,
                 bias=negmax[:],
                 scale=-1.0,
@@ -225,44 +225,56 @@ def tile_single_head_split_window_attention_1d_kernel(
             )
 
         def te(j):
-            eT = ps_e.tile([P, 2, 4, P], BF16, name="eT")
+            eT = ps_e.tile([P, 2, 2, P], F32, name="eT")
+            words = live["e", j][:].rearrange("q a k -> q (a k)").bitcast(F32)
             for a in range(2):
-                for t in range(4):
+                for u in range(2):
                     nc.tensor.transpose(
-                        out=eT[:, a, t, :],
-                        in_=live["e", j][:, a, P * t : P * t + P],
-                        identity=ident[:],
+                        out=eT[:, a, u, :],
+                        in_=words[:, 2 * P * a + P * u : 2 * P * a + P * u + P],
+                        identity=ident_f[:],
                     )
             live["eT", j] = eT
 
         def eve(j, on_vector):
             g_sb = work.tile([P, 2, P, 4], BF16, name="g_sb", align_bytes=64)
+            dst = (
+                g_sb[:]
+                .rearrange("p a q t -> p (a q t)")
+                .bitcast(F32)
+                .rearrange("p (a q u) -> p a q u", a=2, u=2)
+            )
+            src = live["eT", j][:].rearrange("p a u q -> p a q u")
             if on_vector:
-                nc.vector.tensor_copy(
-                    out=g_sb[:], in_=live["eT", j][:].rearrange("p a t q -> p a q t")
-                )
+                nc.vector.tensor_copy(out=dst, in_=src)
             else:
-                nc.scalar.copy(out=g_sb[:], in_=live["eT", j][:].rearrange("p a t q -> p a q t"))
+                nc.scalar.copy(out=dst, in_=src)
             live["g", j] = g_sb
 
         def te_one(i):
-            eT1 = ps_s.tile([P, 4, P], BF16, name="eT1", tag="s_ps")
-            for t in range(4):
+            eT1 = ps_s.tile([P, 2, P], F32, name="eT1", tag="s_ps")
+            words = live["e", i // 2][:].rearrange("q a k -> q (a k)").bitcast(F32)
+            for u in range(2):
+                w0 = 2 * P * (i % 2) + P * u
                 nc.tensor.transpose(
-                    out=eT1[:, t, :],
-                    in_=live["e", i // 2][:, i % 2, P * t : P * t + P],
-                    identity=ident[:],
+                    out=eT1[:, u, :], in_=words[:, w0 : w0 + P], identity=ident_f[:]
                 )
             live["eT1", i] = eT1
 
         def eve_one(i, on_vector):
             if i % 2 == 0:
                 live["g", i // 2] = work.tile([P, 2, P, 4], BF16, name="g_sb", align_bytes=64)
-            dst = live["g", i // 2][:, i % 2, :, :]
+            dst = (
+                live["g", i // 2][:]
+                .rearrange("p a q t -> p (a q t)")
+                .bitcast(F32)[:, 2 * P * (i % 2) : 2 * P * (i % 2) + 2 * P]
+                .rearrange("p (q u) -> p q u", u=2)
+            )
+            src = live["eT1", i][:].rearrange("p u q -> p q u")
             if on_vector:
-                nc.vector.tensor_copy(out=dst, in_=live["eT1", i][:].rearrange("p t q -> p q t"))
+                nc.vector.tensor_copy(out=dst, in_=src)
             else:
-                nc.scalar.copy(out=dst, in_=live["eT1", i][:].rearrange("p t q -> p q t"))
+                nc.scalar.copy(out=dst, in_=src)
 
         def qnt(j):
             u, b = j // 2, j % 2

@@ -145,9 +145,12 @@ def tile_single_head_split_window_attention_1d_kernel(
                 )
             live["t_ps", u] = t_ps
 
-        def evqk(u):
+        def evqk(u, on_vector):
             qkT = work.tile([P, 8, P], BF16, name="qkT")
-            nc.vector.tensor_copy(out=qkT[:], in_=live["t_ps", u][:])
+            if on_vector:
+                nc.vector.tensor_copy(out=qkT[:], in_=live["t_ps", u][:])
+            else:
+                nc.scalar.copy(out=qkT[:], in_=live["t_ps", u][:])
             live["qkT", u] = qkT
 
         def vprep(u):
@@ -337,7 +340,7 @@ def tile_single_head_split_window_attention_1d_kernel(
                 nc.sync.dma_start(out=o_v[:, g, :, :], in_=o_sb[:, 2 * hh : 2 * hh + 2, :])
 
         tqk(0)
-        evqk(0)
+        evqk(0, True)
         bias_t(0, 0, 1, False)
         bias_t(0, 1, 1, False)
         bias_ev(0, 0, 1, True)
@@ -363,8 +366,6 @@ def tile_single_head_split_window_attention_1d_kernel(
             if m >= 0:
                 rowmax(2 * m)
                 rowmax(2 * m + 1)
-            if m >= 0 and m % 2 == 0:
-                evqk(m // 2 + 1)
             if m >= 3:
                 qnt(m - 3)
             if m >= 0 and m % 2 == 0:
@@ -376,6 +377,8 @@ def tile_single_head_split_window_attention_1d_kernel(
                 bias_ev(1, 2 * (s - 3), 2, True)
             if s == 0:
                 bias_ev(0, 2, 2, False)
+            if m >= 0 and m % 2 == 0:
+                evqk(m // 2 + 1, False)
             if m >= 0:
                 expo(2 * m)
                 expo(2 * m + 1)

@@ -107,16 +107,19 @@ def tile_single_head_split_window_attention_1d_kernel(
             nc.tensor.matmul(out=z_ps[:], lhsT=ident[:], rhs=zeros[:], start=True, stop=True)
 
         bp = [const.tile([P, 4, 4, P], F32, name="bp%d" % n) for n in range(NWIN)]
-        v_codes = [const.tile([P, C], U32, name="v_codes%d" % u, align_bytes=64) for u in range(UNITS)]
-        v_scales = [const.tile([P, C], U8, name="v_scales%d" % u, align_bytes=64) for u in range(UNITS)]
+        v_groups = ((0, 1), (1, 1), (2, 2), (4, 4))
+        v_q = {}
+        for u0, nu in v_groups:
+            gv = const.tile([P, nu, C, 4], BF16, name="gv%d" % u0, align_bytes=64)
+            codes = const.tile([P, nu, C], U32, name="v_codes%d" % u0, align_bytes=64)
+            scales = const.tile([P, nu, C], U8, name="v_scales%d" % u0, align_bytes=64)
+            for i in range(nu):
+                v_q[u0 + i] = (gv, codes, scales, i)
 
         live = {}
 
-        def bias_t(n, a0, na, spare):
-            if spare:
-                bT = ps_o.tile([P, na, 4, P], BF16, name="bT", tag="o_ps")
-            else:
-                bT = ps_e.tile([P, na, 4, P], BF16, name="bT", tag="eT")
+        def bias_t(n, a0, na, pool, tag):
+            bT = pool.tile([P, na, 4, P], BF16, name="bT", tag=tag)
             for a in range(na):
                 for t in range(4):
                     nc.tensor.transpose(
@@ -135,41 +138,52 @@ def tile_single_head_split_window_attention_1d_kernel(
             else:
                 nc.scalar.mul(out=bp[n][:, a0 : a0 + na, :, :], in_=bT[:], mul=C ** 0.5)
 
+        def qk_source(u, i):
+            return k_sb[u][:, i, :] if i < 4 else q_sb[u][:, (i - 4) // 2, i % 2, :]
+
         def tqk(u):
             t_ps = ps_t.tile([P, 8, P], BF16, name="t_ps")
-            for t in range(4):
-                nc.tensor.transpose(out=t_ps[:, t, :], in_=k_sb[u][:, t, :], identity=ident[:])
-            for a in range(4):
-                nc.tensor.transpose(
-                    out=t_ps[:, 4 + a, :], in_=q_sb[u][:, a // 2, a % 2, :], identity=ident[:]
-                )
+            for i in range(8):
+                nc.tensor.transpose(out=t_ps[:, i, :], in_=qk_source(u, i), identity=ident[:])
             live["t_ps", u] = t_ps
 
-        def evqk(u, on_vector):
+        def evqk(u):
             qkT = work.tile([P, 8, P], BF16, name="qkT")
-            if on_vector:
-                nc.vector.tensor_copy(out=qkT[:], in_=live["t_ps", u][:])
-            else:
-                nc.scalar.copy(out=qkT[:], in_=live["t_ps", u][:])
+            nc.scalar.copy(
+                out=qkT[:].rearrange("p i x -> p (i x)").bitcast(F32),
+                in_=live["t_ps", u][:].rearrange("p i x -> p (i x)").bitcast(F32),
+            )
             live["qkT", u] = qkT
 
+        def first_qk():
+            qkT = work.tile([P, 8, P], BF16, name="qkT")
+            t_k = ps_t.tile([P, 4, P], BF16, name="t_k", tag="t_ps")
+            t_q = ps_s.tile([P, 4, P], BF16, name="t_q", tag="s_ps")
+            for i in range(4):
+                nc.tensor.transpose(out=t_k[:, i, :], in_=qk_source(0, i), identity=ident[:])
+            for i in range(4):
+                nc.tensor.transpose(out=t_q[:, i, :], in_=qk_source(0, 4 + i), identity=ident[:])
+            nc.vector.tensor_copy(out=qkT[:, 0:4, :], in_=t_k[:])
+            nc.scalar.copy(out=qkT[:, 4:8, :], in_=t_q[:])
+            live["qkT", 0] = qkT
+
         def vprep(u):
-            gv = work.tile([P, C, 4], BF16, name="gv", align_bytes=64)
+            gv, codes, scales, i = v_q[u]
             nc.gpsimd.tensor_scalar(
-                out=gv[:],
+                out=gv[:, i],
                 in0=v_sb[u][:].rearrange("p t c -> p c t"),
                 scalar1=1.0,
                 scalar2=0.0,
                 op0=ALU.mult,
                 op1=ALU.add,
             )
-            live["gv", u] = gv
 
-        def vquant(u):
+        def vquant(u0):
+            gv, codes, scales, i = v_q[u0]
             nc.vector.quantize_mx(
-                out=v_codes[u][:].bitcast(FP8X4),
-                scales=v_scales[u][:],
-                in_=live["gv", u][:].rearrange("p c t -> p (c t)"),
+                out=codes[:].rearrange("p u c -> p (u c)").bitcast(FP8X4),
+                scales=scales[:].rearrange("p u c -> p (u c)"),
+                in_=gv[:].rearrange("p u c t -> p (u c t)"),
             )
 
         def qk(i):
@@ -239,20 +253,20 @@ def tile_single_head_split_window_attention_1d_kernel(
                     )
             live["eT", j] = eT
 
+        def g_words(i, na):
+            u, a = i // 4, i % 4
+            if a == 0:
+                live["g", u] = work.tile([P, 4 * P * 4], BF16, name="g_sb", align_bytes=64)
+            words = live["g", u][:].bitcast(F32)[:, 2 * P * a : 2 * P * (a + na)]
+            return words.rearrange("p (a q u) -> p a q u", a=na, u=2)
+
         def eve(j, on_vector):
-            g_sb = work.tile([P, 2, P, 4], BF16, name="g_sb", align_bytes=64)
-            dst = (
-                g_sb[:]
-                .rearrange("p a q t -> p (a q t)")
-                .bitcast(F32)
-                .rearrange("p (a q u) -> p a q u", a=2, u=2)
-            )
+            dst = g_words(2 * j, 2)
             src = live["eT", j][:].rearrange("p a u q -> p a q u")
             if on_vector:
                 nc.vector.tensor_copy(out=dst, in_=src)
             else:
                 nc.scalar.copy(out=dst, in_=src)
-            live["g", j] = g_sb
 
         def te_one(i):
             eT1 = ps_s.tile([P, 2, P], F32, name="eT1", tag="s_ps")
@@ -265,100 +279,93 @@ def tile_single_head_split_window_attention_1d_kernel(
             live["eT1", i] = eT1
 
         def eve_one(i, on_vector):
-            if i % 2 == 0:
-                live["g", i // 2] = work.tile([P, 2, P, 4], BF16, name="g_sb", align_bytes=64)
-            dst = (
-                live["g", i // 2][:]
-                .rearrange("p a q t -> p (a q t)")
-                .bitcast(F32)[:, 2 * P * (i % 2) : 2 * P * (i % 2) + 2 * P]
-                .rearrange("p (q u) -> p q u", u=2)
-            )
-            src = live["eT1", i][:].rearrange("p u q -> p q u")
+            dst = g_words(i, 1)
+            src = live["eT1", i][:].rearrange("p u q -> p q u").unsqueeze(1)
             if on_vector:
                 nc.vector.tensor_copy(out=dst, in_=src)
             else:
                 nc.scalar.copy(out=dst, in_=src)
 
-        def qnt(j):
-            u, b = j // 2, j % 2
-            if b == 0:
+        def qnt(u, a0, na):
+            if a0 == 0:
                 live["c", u] = (
                     work.tile([P, 4 * P], U32, name="e_codes", align_bytes=64),
                     work.tile([P, 4 * P], U8, name="e_scales", align_bytes=64),
                 )
             e_codes, e_scales = live["c", u]
             nc.vector.quantize_mx(
-                out=e_codes[:, 2 * P * b : 2 * P * b + 2 * P].bitcast(FP8X4),
-                scales=e_scales[:, 2 * P * b : 2 * P * b + 2 * P],
-                in_=live["g", j][:].rearrange("p a q t -> p (a q t)"),
+                out=e_codes[:, P * a0 : P * (a0 + na)].bitcast(FP8X4),
+                scales=e_scales[:, P * a0 : P * (a0 + na)],
+                in_=live["g", u][:, 4 * P * a0 : 4 * P * (a0 + na)],
             )
 
-        def mxu(u, spare):
+        def mx(u, a0, na, pool, tag):
             e_codes, e_scales = live["c", u]
-            if spare:
-                o_ps = ps_s.tile([P, 4, C], F32, name="o_ps", tag="s_ps")
-            else:
-                o_ps = ps_o.tile([P, 4, C], F32, name="o_ps")
-            for a in range(4):
+            gv, v_codes, v_scales, i = v_q[u]
+            o_ps = pool.tile([P, na, C], F32, name="o_ps", tag=tag)
+            for a in range(na):
+                c0 = P * (a0 + a)
                 nc.tensor.matmul_mx(
                     out=o_ps[:, a, :],
-                    lhsT=e_codes[:, P * a : P * a + P].bitcast(FP8X4),
-                    lhsT_scale=e_scales[:, P * a : P * a + P],
-                    rhs=v_codes[u][:].bitcast(FP8X4),
-                    rhs_scale=v_scales[u][:],
+                    lhsT=e_codes[:, c0 : c0 + P].bitcast(FP8X4),
+                    lhsT_scale=e_scales[:, c0 : c0 + P],
+                    rhs=v_codes[:, i, :].bitcast(FP8X4),
+                    rhs_scale=v_scales[:, i, :],
                     start=True,
                     stop=True,
                 )
-            live["o", u] = o_ps
+            live["o", u, a0] = o_ps
 
         def recip(u):
             rinv = stat.tile([P, 4], F32, name="rinv")
             nc.vector.reciprocal(out=rinv[:], in_=live["rowsum", u][:])
             live["rinv", u] = rinv
 
-        def outu(u, on_vector):
+        def outs(u, a0, na, on_vector):
             r, n = u % ROWS, u // ROWS
             rinv = live["rinv", u]
-            o_sb = work.tile([P, 4, C], F32, name="o_sb")
+            o_ps = live["o", u, a0]
+            o_sb = work.tile([P, na, C], F32, name="o_sb")
             if on_vector:
                 nc.vector.tensor_tensor(
                     out=o_sb[:],
-                    in0=live["o", u][:],
-                    in1=rinv[:].unsqueeze(2).to_broadcast([P, 4, C]),
+                    in0=o_ps[:],
+                    in1=rinv[:, a0 : a0 + na].unsqueeze(2).to_broadcast([P, na, C]),
                     op=ALU.mult,
                 )
             else:
-                for a in range(4):
+                for a in range(na):
                     nc.scalar.activation(
                         out=o_sb[:, a, :],
-                        in_=live["o", u][:, a, :],
+                        in_=o_ps[:, a, :],
                         func=ACT.Copy,
-                        scale=rinv[:, a : a + 1],
+                        scale=rinv[:, a0 + a : a0 + a + 1],
                     )
-            for hh in range(2):
+            for b in range(na // 2):
+                hh = a0 // 2 + b
                 g = 4 * r + (1 + 2 * n + hh) % 4
-                nc.sync.dma_start(out=o_v[:, g, :, :], in_=o_sb[:, 2 * hh : 2 * hh + 2, :])
+                nc.sync.dma_start(out=o_v[:, g, :, :], in_=o_sb[:, 2 * b : 2 * b + 2, :])
 
-        tqk(0)
-        evqk(0, True)
-        bias_t(0, 0, 1, False)
-        bias_t(0, 1, 1, False)
+        first_qk()
+        bias_t(0, 0, 1, ps_e, "eT")
+        bias_t(0, 1, 1, ps_e, "eT")
+        bias_t(0, 2, 1, ps_o, "o_ps")
+        bias_t(0, 3, 1, ps_s, "s_ps")
         bias_ev(0, 0, 1, True)
         bias_ev(0, 1, 1, False)
+        bias_ev(0, 2, 1, True)
+        bias_ev(0, 3, 1, False)
 
-        for s in range(PAIRS - 1):
+        for s in range(PAIRS):
             m = s - 1
-            unit_out = (s - 6) // 2 if s % 2 == 0 else -1
-            if s in (3, 4):
-                bias_t(1, 2 * (s - 3), 2, True)
             qk(2 * s)
             qk(2 * s + 1)
+            if s >= 5 and s % 2 == 1:
+                mx((s - 5) // 2, 0, 4, ps_o, "o_ps")
             addbias(2 * s)
             addbias(2 * s + 1)
-            if unit_out >= 0:
-                mxu(unit_out, False)
-            if s == 0:
-                bias_t(0, 2, 2, True)
+            if s in (2, 3):
+                bias_t(1, 2 * (s - 2), 2, ps_o, "o_ps")
             if s % 2 == 0 and s // 2 + 1 < UNITS:
                 tqk(s // 2 + 1)
             if s >= 2:
@@ -366,61 +373,43 @@ def tile_single_head_split_window_attention_1d_kernel(
             if m >= 0:
                 rowmax(2 * m)
                 rowmax(2 * m + 1)
-            if m >= 3:
-                qnt(m - 3)
-            if m >= 0 and m % 2 == 0:
-                vquant(m // 2)
-            if unit_out >= 0:
-                recip(unit_out)
-                outu(unit_out, True)
-            if s in (3, 4):
-                bias_ev(1, 2 * (s - 3), 2, True)
-            if s == 0:
-                bias_ev(0, 2, 2, False)
-            if m >= 0 and m % 2 == 0:
-                evqk(m // 2 + 1, False)
+            if s >= 4 and s % 2 == 0:
+                qnt((s - 4) // 2, 0, 4)
+            if s in (1, 2, 5, 9):
+                vquant({1: 0, 2: 1, 5: 2, 9: 4}[s])
+            if s >= 5 and s % 2 == 1:
+                recip((s - 5) // 2)
+                outs((s - 5) // 2, 0, 4, True)
+            if s in (2, 3):
+                bias_ev(1, 2 * (s - 2), 2, True)
+            if m >= 0 and m % 2 == 0 and m // 2 + 1 < UNITS:
+                evqk(m // 2 + 1)
             if m >= 0:
                 expo(2 * m)
                 expo(2 * m + 1)
             if m >= 1:
                 eve(m - 1, False)
-            if s % 2 == 0:
-                vprep(s // 2)
+            if s < UNITS:
+                vprep(s)
 
-        qk(30)
-        qk(31)
-        addbias(30)
-        addbias(31)
-        te(13)
-        rowmax(28)
-        rowmax(29)
-        qnt(11)
-        vquant(7)
-        expo(28)
-        expo(29)
-
-        mxu(5, False)
         te(14)
         rowmax(30)
         rowmax(31)
         expo(30)
         expo(31)
+        qnt(6, 0, 4)
+        mx(6, 0, 4, ps_o, "o_ps")
         te_one(30)
         te_one(31)
-        eve(13, True)
-        qnt(12)
-        recip(5)
-        outu(5, True)
-        qnt(13)
-        eve_one(30, True)
-        eve(14, False)
-        eve_one(31, False)
-
-        mxu(6, False)
+        eve(14, True)
         recip(6)
-        qnt(14)
-        qnt(15)
+        qnt(7, 0, 2)
+        outs(6, 0, 4, False)
         recip(7)
-        outu(6, False)
-        mxu(7, True)
-        outu(7, True)
+        eve_one(30, True)
+        mx(7, 0, 2, ps_s, "s_ps")
+        eve_one(31, False)
+        outs(7, 0, 2, True)
+        qnt(7, 2, 2)
+        mx(7, 2, 2, ps_s, "s_ps")
+        outs(7, 2, 2, True)

@@ -70,15 +70,21 @@ def tile_single_head_split_window_attention_1d_kernel(
 
         def load_v(u):
             r, n = u % ROWS, u // ROWS
-            for hh in range(2):
-                nc.sync.dma_start(
-                    out=v_sb[u][64 * hh : 64 * hh + 64],
-                    in_=v_v[4 * r + (1 + 2 * n + hh) % 4],
-                )
+            if n == 0:
+                r0 = 4 * WIN // 2 * r + WIN // 2
+                src = v.flatten_outer_dims()[r0 : r0 + WIN, :]
+                nc.sync.dma_start(out=v_sb[u][:], in_=src.rearrange("(p t) c -> p t c", t=4))
+            else:
+                for hh in range(2):
+                    nc.sync.dma_start(
+                        out=v_sb[u][64 * hh : 64 * hh + 64],
+                        in_=v_v[4 * r + (3 + hh) % 4],
+                    )
 
         def load_bias(n):
             for hh in range(2):
-                nc.sync.dma_start(out=b_sb[n][hh][:], in_=b_v[:, n, hh])
+                for j in range(2):
+                    nc.sync.dma_start(out=b_sb[n][hh][:, j], in_=b_v[:, n, hh, j])
 
         for u in range(UNITS):
             load_tiles(k_sb[u], k_v, u)
@@ -212,7 +218,7 @@ def tile_single_head_split_window_attention_1d_kernel(
                 )
 
         def rowmax(i):
-            sp = work.tile([P, 2, P, 2], F32, name="sp")
+            sp = stat.tile([P, 2, P, 2], F32, name="sp")
             negmax = stat.tile([P, 1], F32, name="negmax")
             nc.vector.tensor_scalar(
                 out=sp[:],
@@ -349,51 +355,61 @@ def tile_single_head_split_window_attention_1d_kernel(
         first_qk()
         bias_t(0, 0, 1, ps_e, "eT")
         bias_t(0, 1, 1, ps_e, "eT")
-        bias_t(0, 2, 1, ps_o, "o_ps")
-        bias_t(0, 3, 1, ps_s, "s_ps")
         bias_ev(0, 0, 1, True)
         bias_ev(0, 1, 1, False)
-        bias_ev(0, 2, 1, True)
-        bias_ev(0, 3, 1, False)
+        qk(0)
+        qk(1)
+        bias_t(0, 2, 1, ps_o, "o_ps")
+        bias_ev(0, 2, 1, False)
+        addbias(0)
+        addbias(1)
+        bias_t(0, 3, 1, ps_e, "eT")
+        tqk(1)
+        rowmax(0)
+        rowmax(1)
+        bias_ev(0, 3, 1, True)
 
-        for s in range(PAIRS):
+        for s in range(1, PAIRS):
             m = s - 1
-            qk(2 * s)
-            qk(2 * s + 1)
-            if s >= 5 and s % 2 == 1:
-                mx((s - 5) // 2, 0, 4, ps_o, "o_ps")
-            addbias(2 * s)
-            addbias(2 * s + 1)
-            if s in (2, 3):
-                bias_t(1, 2 * (s - 2), 2, ps_o, "o_ps")
-            if s % 2 == 0 and s // 2 + 1 < UNITS:
-                tqk(s // 2 + 1)
-            if s >= 2:
-                te(s - 2)
-            if m >= 0:
+            if s <= UNITS:
+                vprep(s - 1)
+            if m >= 1:
                 rowmax(2 * m)
+                if s >= 4 and s % 2 == 0:
+                    recip((s - 4) // 2)
                 rowmax(2 * m + 1)
+            if s in (2, 3):
+                bias_ev(1, 2 * (s - 2), 2, True)
             if s >= 4 and s % 2 == 0:
                 qnt((s - 4) // 2, 0, 4)
             if s in (1, 2, 5, 9):
                 vquant({1: 0, 2: 1, 5: 2, 9: 4}[s])
+            qk(2 * s)
             if s >= 5 and s % 2 == 1:
-                recip((s - 5) // 2)
+                mx((s - 5) // 2, 0, 4, ps_o, "o_ps")
+            qk(2 * s + 1)
+            addbias(2 * s)
+            addbias(2 * s + 1)
+            if s >= 2:
+                te(s - 2)
+            if s % 2 == 0 and s // 2 + 1 < UNITS:
+                tqk(s // 2 + 1)
+            if s in (1, 2):
+                bias_t(1, 2 * (s - 1), 2, ps_o, "o_ps")
+            if s >= 5 and s % 2 == 1:
                 outs((s - 5) // 2, 0, 4, True)
-            if s in (2, 3):
-                bias_ev(1, 2 * (s - 2), 2, True)
-            if m >= 0 and m % 2 == 0 and m // 2 + 1 < UNITS:
+            if m % 2 == 0 and m // 2 + 1 < UNITS and s > 1:
                 evqk(m // 2 + 1)
-            if m >= 0:
-                expo(2 * m)
-                expo(2 * m + 1)
+            expo(2 * m)
+            expo(2 * m + 1)
+            if s == 1:
+                evqk(1)
             if m >= 1:
                 eve(m - 1, False)
-            if s < UNITS:
-                vprep(s)
 
         te(14)
         rowmax(30)
+        recip(6)
         rowmax(31)
         expo(30)
         expo(31)
@@ -402,14 +418,13 @@ def tile_single_head_split_window_attention_1d_kernel(
         te_one(30)
         te_one(31)
         eve(14, True)
-        recip(6)
-        qnt(7, 0, 2)
-        outs(6, 0, 4, False)
         recip(7)
         eve_one(30, True)
-        mx(7, 0, 2, ps_s, "s_ps")
         eve_one(31, False)
-        outs(7, 0, 2, True)
+        qnt(7, 0, 2)
+        mx(7, 0, 2, ps_s, "s_ps")
         qnt(7, 2, 2)
         mx(7, 2, 2, ps_s, "s_ps")
+        outs(6, 0, 4, False)
+        outs(7, 0, 2, True)
         outs(7, 2, 2, True)

@@ -30,6 +30,7 @@ def tile_single_head_split_window_attention_1d_kernel(
 
     q_v = q.flatten_outer_dims().rearrange("(g p j) c -> p g j c", p=P, j=2)
     k_v = k.flatten_outer_dims().rearrange("(t p) c -> p t c", p=P)
+    k_w = k.flatten_outer_dims().rearrange("(g p e) c -> g p e c", p=P, e=2)
     v_v = v.flatten_outer_dims().rearrange("(g p t) c -> g p t c", p=P // 2, t=4)
     b_v = attn_mask.rearrange("n (h p j) k -> p n h j k", p=P, j=2)
     o_v = out.flatten_outer_dims().rearrange("(g p j) c -> p g j c", p=P, j=2)
@@ -52,13 +53,13 @@ def tile_single_head_split_window_attention_1d_kernel(
             for n in range(NWIN)
         ]
 
-        def load_tiles(dst, src, u):
+        def load_k(u):
             r, n = u % ROWS, u // ROWS
             if n == 0:
-                nc.sync.dma_start(out=dst[:], in_=src[:, 8 * r + 2 : 8 * r + 6, :])
+                nc.sync.dma_start(out=k_sb[u][:], in_=k_v[:, 8 * r + 2 : 8 * r + 6, :])
             else:
-                nc.sync.dma_start(out=dst[:, 0:2, :], in_=src[:, 8 * r + 6 : 8 * r + 8, :])
-                nc.sync.dma_start(out=dst[:, 2:4, :], in_=src[:, 8 * r : 8 * r + 2, :])
+                nc.sync.dma_start(out=k_sb[u][:, 0:2, :], in_=k_w[4 * r + 3])
+                nc.sync.dma_start(out=k_sb[u][:, 2:4, :], in_=k_w[4 * r])
 
         def load_q(u):
             r, n = u % ROWS, u // ROWS
@@ -87,7 +88,7 @@ def tile_single_head_split_window_attention_1d_kernel(
                     nc.sync.dma_start(out=b_sb[n][hh][:, j], in_=b_v[:, n, hh, j])
 
         for u in range(UNITS):
-            load_tiles(k_sb[u], k_v, u)
+            load_k(u)
             load_q(u)
             if u == 0:
                 load_bias(0)
@@ -144,6 +145,38 @@ def tile_single_head_split_window_attention_1d_kernel(
             else:
                 nc.scalar.mul(out=bp[n][:, a0 : a0 + na, :, :], in_=bT[:], mul=C ** 0.5)
 
+        def bias_w(a0):
+            bT = ps_o.tile([P, 2, 2, P], F32, name="bTw", tag="o_ps")
+            for a in range(2):
+                words = b_sb[1][a0 // 2][:, a, :].bitcast(F32)
+                for u in range(2):
+                    nc.tensor.transpose(
+                        out=bT[:, a, u, :],
+                        in_=words[:, P * u : P * u + P],
+                        identity=ident_f[:],
+                    )
+            live["bTw", a0] = bT
+
+        def bias_w_copy(a0):
+            bw = const.tile([P, 2 * 2 * P * 2], BF16, name="bw%d" % a0)
+            nc.vector.tensor_copy(
+                out=bw[:].bitcast(F32),
+                in_=live["bTw", a0][:].rearrange("p a u q -> p (a u q)"),
+            )
+            live["bw", a0] = bw
+
+        def bias_w_spread(a):
+            bw = live["bw", a // 2 * 2]
+            src = bw[:, 4 * P * (a % 2) : 4 * P * (a % 2) + 4 * P]
+            nc.gpsimd.tensor_scalar(
+                out=bp[1][:, a, :, :].rearrange("p (u e) q -> p u e q", e=2),
+                in0=src.rearrange("p (u q e) -> p u e q", u=2, e=2),
+                scalar1=C ** 0.5,
+                scalar2=0.0,
+                op0=ALU.mult,
+                op1=ALU.add,
+            )
+
         def qk_source(u, i):
             return k_sb[u][:, i, :] if i < 4 else q_sb[u][:, (i - 4) // 2, i % 2, :]
 
@@ -192,7 +225,7 @@ def tile_single_head_split_window_attention_1d_kernel(
                 in_=gv[:].rearrange("p u c t -> p (u c t)"),
             )
 
-        def qk(i):
+        def qk(i, alone=False):
             u, a = i // 4, i % 4
             qkT = live["qkT", u]
             s_ps = ps_s.tile([P, WIN], F32, name="s_ps")
@@ -201,7 +234,7 @@ def tile_single_head_split_window_attention_1d_kernel(
                 lhsT=qkT[:, 4 + a, :],
                 rhs=qkT[:, 0:4, :].rearrange("p t k -> p (t k)"),
                 start=True,
-                stop=False,
+                stop=alone,
             )
             live["s_ps", i] = s_ps
 
@@ -218,18 +251,42 @@ def tile_single_head_split_window_attention_1d_kernel(
                 )
 
         def rowmax(i):
-            sp = stat.tile([P, 2, P, 2], F32, name="sp")
+            sp = stat.tile([P, WIN], F32, name="sp")
             negmax = stat.tile([P, 1], F32, name="negmax")
+            if i // 4 < ROWS:
+                src = live["s_ps", i][:]
+                dst = sp[:]
+            else:
+                src = live["s_ps", i][:].rearrange("q (u e x) -> q u x e", u=2, e=2)
+                dst = sp[:].rearrange("q (u x e) -> q u x e", u=2, e=2)
             nc.vector.tensor_scalar(
-                out=sp[:],
-                in0=live["s_ps", i][:].rearrange("q (p u e) -> q u p e", u=2, e=2),
+                out=dst,
+                in0=src,
                 scalar1=-scale,
                 scalar2=None,
                 op0=ALU.mult,
                 op1=ALU.min,
                 accum_out=negmax[:],
             )
-            live["sp", i] = (sp, negmax)
+            live["sp", i] = (sp, negmax, -1.0)
+
+        def biased(i):
+            sp = stat.tile([P, WIN], F32, name="sp")
+            nc.vector.scalar_tensor_tensor(
+                out=sp[:],
+                in0=live["s_ps", i][:],
+                scalar=scale,
+                in1=b_sb[0][0][:, i, :],
+                op0=ALU.mult,
+                op1=ALU.add,
+            )
+            live["biased", i] = sp
+
+        def biased_max(i):
+            sp = live["biased", i]
+            negmax = stat.tile([P, 1], F32, name="negmax")
+            nc.vector.reduce_max(out=negmax[:], in_=sp[:], axis=mybir.AxisListType.X, negate=True)
+            live["sp", i] = (sp, negmax, 1.0)
 
         def expo(i):
             u, a = i // 4, i % 4
@@ -237,13 +294,13 @@ def tile_single_head_split_window_attention_1d_kernel(
                 live["rowsum", u] = stat.tile([P, 4], F32, name="rowsum")
             if a % 2 == 0:
                 live["e", i // 2] = work.tile([P, 2, WIN], BF16, name="e_sb")
-            sp, negmax = live["sp", i]
+            sp, negmax, sign = live["sp", i]
             nc.scalar.activation(
-                out=live["e", i // 2][:, a % 2, :],
-                in_=sp[:].rearrange("q u p e -> q (u p e)"),
+                out=live["e", i // 2][:, a % 2, :].rearrange("q (u p e) -> q u p e", u=2, e=2),
+                in_=sp[:].rearrange("q (p u e) -> q u p e", u=2, e=2),
                 func=ACT.Exp,
                 bias=negmax[:],
-                scale=-1.0,
+                scale=sign,
                 accum_out=live["rowsum", u][:, a : a + 1],
             )
 
@@ -357,35 +414,38 @@ def tile_single_head_split_window_attention_1d_kernel(
         bias_t(0, 1, 1, ps_e, "eT")
         bias_ev(0, 0, 1, True)
         bias_ev(0, 1, 1, False)
-        qk(0)
-        qk(1)
+        qk(0, True)
+        qk(1, True)
         bias_t(0, 2, 1, ps_o, "o_ps")
         bias_ev(0, 2, 1, False)
-        addbias(0)
-        addbias(1)
         bias_t(0, 3, 1, ps_e, "eT")
+        bias_ev(0, 3, 1, False)
         tqk(1)
-        rowmax(0)
-        rowmax(1)
-        bias_ev(0, 3, 1, True)
+        evqk(1)
+        biased(0)
+        biased(1)
+        biased_max(0)
+        biased_max(1)
 
         for s in range(1, PAIRS):
             m = s - 1
             if s <= UNITS:
                 vprep(s - 1)
+            if 4 <= s <= 7:
+                bias_w_spread(s - 4)
             if m >= 1:
                 rowmax(2 * m)
                 if s >= 4 and s % 2 == 0:
                     recip((s - 4) // 2)
                 rowmax(2 * m + 1)
             if s in (2, 3):
-                bias_ev(1, 2 * (s - 2), 2, True)
+                bias_w_copy(2 * (s - 2))
             if s >= 4 and s % 2 == 0:
                 qnt((s - 4) // 2, 0, 4)
-            if s in (1, 2, 5, 9):
-                vquant({1: 0, 2: 1, 5: 2, 9: 4}[s])
+            if s in (3, 4, 6, 10):
+                vquant({3: 0, 4: 1, 6: 2, 10: 4}[s])
             qk(2 * s)
-            if s >= 5 and s % 2 == 1:
+            if s >= 5 and s % 2 == 1 and s < PAIRS - 1:
                 mx((s - 5) // 2, 0, 4, ps_o, "o_ps")
             qk(2 * s + 1)
             addbias(2 * s)
@@ -395,28 +455,28 @@ def tile_single_head_split_window_attention_1d_kernel(
             if s % 2 == 0 and s // 2 + 1 < UNITS:
                 tqk(s // 2 + 1)
             if s in (1, 2):
-                bias_t(1, 2 * (s - 1), 2, ps_o, "o_ps")
-            if s >= 5 and s % 2 == 1:
+                bias_w(2 * (s - 1))
+            if s >= 5 and s % 2 == 1 and s < PAIRS - 1:
                 outs((s - 5) // 2, 0, 4, True)
             if m % 2 == 0 and m // 2 + 1 < UNITS and s > 1:
                 evqk(m // 2 + 1)
             expo(2 * m)
             expo(2 * m + 1)
-            if s == 1:
-                evqk(1)
             if m >= 1:
                 eve(m - 1, False)
 
+        mx(5, 0, 4, ps_o, "o_ps")
         te(14)
         rowmax(30)
-        recip(6)
         rowmax(31)
         expo(30)
         expo(31)
-        qnt(6, 0, 4)
-        mx(6, 0, 4, ps_o, "o_ps")
         te_one(30)
         te_one(31)
+        recip(6)
+        outs(5, 0, 4, True)
+        qnt(6, 0, 4)
+        mx(6, 0, 4, ps_o, "o_ps")
         eve(14, True)
         recip(7)
         eve_one(30, True)

@@ -29,8 +29,7 @@ def tile_single_head_split_window_attention_1d_kernel(
     scale = 1.0 / (C ** 0.5)
 
     q_v = q.flatten_outer_dims().rearrange("(g p j) c -> p g j c", p=P, j=2)
-    k_v = k.flatten_outer_dims().rearrange("(t p) c -> p t c", p=P)
-    k_w = k.flatten_outer_dims().rearrange("(g p e) c -> g p e c", p=P, e=2)
+    k_v = k.flatten_outer_dims().rearrange("(g p e) c -> p g e c", p=P, e=2)
     v_v = v.flatten_outer_dims().rearrange("(g p t) c -> g p t c", p=P // 2, t=4)
     b_v = attn_mask.rearrange("n (h p j) k -> p n h j k", p=P, j=2)
     o_v = out.flatten_outer_dims().rearrange("(g p j) c -> p g j c", p=P, j=2)
@@ -45,7 +44,7 @@ def tile_single_head_split_window_attention_1d_kernel(
         ps_o = ctx.enter_context(tc.psum_pool(name="ps_o", bufs=1))
         ctx.enter_context(tc.manual_schedule())
 
-        k_sb = [const.tile([P, 4, C], BF16, name="k_sb%d" % u) for u in range(UNITS)]
+        k_sb = [const.tile([P, 2, 2, C], BF16, name="k_sb%d" % u) for u in range(UNITS)]
         q_sb = [const.tile([P, 2, 2, C], BF16, name="q_sb%d" % u) for u in range(UNITS)]
         v_sb = [const.tile([P, 4, C], BF16, name="v_sb%d" % u) for u in range(UNITS)]
         b_sb = [
@@ -56,10 +55,10 @@ def tile_single_head_split_window_attention_1d_kernel(
         def load_k(u):
             r, n = u % ROWS, u // ROWS
             if n == 0:
-                nc.sync.dma_start(out=k_sb[u][:], in_=k_v[:, 8 * r + 2 : 8 * r + 6, :])
+                nc.sync.dma_start(out=k_sb[u][:], in_=k_v[:, 4 * r + 1 : 4 * r + 3, :, :])
             else:
-                nc.sync.dma_start(out=k_sb[u][:, 0:2, :], in_=k_w[4 * r + 3])
-                nc.sync.dma_start(out=k_sb[u][:, 2:4, :], in_=k_w[4 * r])
+                nc.sync.dma_start(out=k_sb[u][:, 0], in_=k_v[:, 4 * r + 3, :, :])
+                nc.sync.dma_start(out=k_sb[u][:, 1], in_=k_v[:, 4 * r, :, :])
 
         def load_q(u):
             r, n = u % ROWS, u // ROWS
@@ -88,8 +87,12 @@ def tile_single_head_split_window_attention_1d_kernel(
                     nc.sync.dma_start(out=b_sb[n][hh][:, j], in_=b_v[:, n, hh, j])
 
         for u in range(UNITS):
-            load_k(u)
-            load_q(u)
+            if u == 0:
+                load_q(u)
+                load_k(u)
+            else:
+                load_k(u)
+                load_q(u)
             if u == 0:
                 load_bias(0)
             else:
@@ -126,59 +129,49 @@ def tile_single_head_split_window_attention_1d_kernel(
         live = {}
 
         def bias_t(n, a0, na, pool, tag):
-            bT = pool.tile([P, na, 4, P], BF16, name="bT", tag=tag)
+            bT = pool.tile([P, na, 2, P], F32, name="bT", tag=tag)
             for a in range(na):
-                for t in range(4):
-                    nc.tensor.transpose(
-                        out=bT[:, a, t, :],
-                        in_=b_sb[n][(a0 + a) // 2][:, (a0 + a) % 2, P * t : P * t + P],
-                        identity=ident[:],
-                    )
-            live["bT", n, a0] = bT
-
-        def bias_ev(n, a0, na, on_vector):
-            bT = live["bT", n, a0]
-            if on_vector:
-                nc.vector.tensor_scalar_mul(
-                    out=bp[n][:, a0 : a0 + na, :, :], in0=bT[:], scalar1=C ** 0.5
-                )
-            else:
-                nc.scalar.mul(out=bp[n][:, a0 : a0 + na, :, :], in_=bT[:], mul=C ** 0.5)
-
-        def bias_w(a0):
-            bT = ps_o.tile([P, 2, 2, P], F32, name="bTw", tag="o_ps")
-            for a in range(2):
-                words = b_sb[1][a0 // 2][:, a, :].bitcast(F32)
+                words = b_sb[n][(a0 + a) // 2][:, (a0 + a) % 2, :].bitcast(F32)
                 for u in range(2):
                     nc.tensor.transpose(
                         out=bT[:, a, u, :],
                         in_=words[:, P * u : P * u + P],
                         identity=ident_f[:],
                     )
-            live["bTw", a0] = bT
+            live["bT", n, a0] = bT
 
-        def bias_w_copy(a0):
-            bw = const.tile([P, 2 * 2 * P * 2], BF16, name="bw%d" % a0)
-            nc.vector.tensor_copy(
-                out=bw[:].bitcast(F32),
-                in_=live["bTw", a0][:].rearrange("p a u q -> p (a u q)"),
-            )
-            live["bw", a0] = bw
+        def bias_copy(n, a0, na, on_vector):
+            bw = const.tile([P, na * 2 * P * 2], BF16, name="bw%d%d" % (n, a0))
+            dst = bw[:].bitcast(F32)
+            src = live["bT", n, a0][:].rearrange("p a u q -> p (a u q)")
+            if on_vector:
+                nc.vector.tensor_copy(out=dst, in_=src)
+            else:
+                nc.scalar.copy(out=dst, in_=src)
+            for a in range(na):
+                live["bw", n, a0 + a] = bw[:, 4 * P * a : 4 * P * a + 4 * P]
 
-        def bias_w_spread(a):
-            bw = live["bw", a // 2 * 2]
-            src = bw[:, 4 * P * (a % 2) : 4 * P * (a % 2) + 4 * P]
+        def bias_spread(n, a):
             nc.gpsimd.tensor_scalar(
-                out=bp[1][:, a, :, :].rearrange("p (u e) q -> p u e q", e=2),
-                in0=src.rearrange("p (u q e) -> p u e q", u=2, e=2),
+                out=bp[n][:, a, :, :].rearrange("p (u e) q -> p u e q", e=2),
+                in0=live["bw", n, a].rearrange("p (u q e) -> p u e q", u=2, e=2),
                 scalar1=C ** 0.5,
                 scalar2=0.0,
                 op0=ALU.mult,
                 op1=ALU.add,
             )
 
+        def bias_direct(n, a):
+            pairs = live["bT", n, a][:].rearrange("p a u q -> p (a u q)").bitcast(BF16)
+            nc.scalar.mul(
+                out=bp[n][:, a, :, :].rearrange("p (u e) q -> p u e q", e=2),
+                in_=pairs.rearrange("p (u q e) -> p u e q", u=2, e=2),
+                mul=C ** 0.5,
+            )
+
         def qk_source(u, i):
-            return k_sb[u][:, i, :] if i < 4 else q_sb[u][:, (i - 4) // 2, i % 2, :]
+            src = k_sb[u] if i < 4 else q_sb[u]
+            return src[:, i % 4 // 2, i % 2, :]
 
         def tqk(u):
             t_ps = ps_t.tile([P, 8, P], BF16, name="t_ps")
@@ -196,14 +189,18 @@ def tile_single_head_split_window_attention_1d_kernel(
 
         def first_qk():
             qkT = work.tile([P, 8, P], BF16, name="qkT")
-            t_k = ps_t.tile([P, 4, P], BF16, name="t_k", tag="t_ps")
             t_q = ps_s.tile([P, 4, P], BF16, name="t_q", tag="s_ps")
-            for i in range(4):
-                nc.tensor.transpose(out=t_k[:, i, :], in_=qk_source(0, i), identity=ident[:])
+            t_k0 = ps_t.tile([P, 2, P], BF16, name="t_k0", tag="t_ps")
+            t_k1 = ps_o.tile([P, 2, P], BF16, name="t_k1", tag="o_ps")
             for i in range(4):
                 nc.tensor.transpose(out=t_q[:, i, :], in_=qk_source(0, 4 + i), identity=ident[:])
-            nc.vector.tensor_copy(out=qkT[:, 0:4, :], in_=t_k[:])
+            for i in range(2):
+                nc.tensor.transpose(out=t_k0[:, i, :], in_=qk_source(0, i), identity=ident[:])
+            for i in range(2):
+                nc.tensor.transpose(out=t_k1[:, i, :], in_=qk_source(0, 2 + i), identity=ident[:])
             nc.scalar.copy(out=qkT[:, 4:8, :], in_=t_q[:])
+            nc.vector.tensor_copy(out=qkT[:, 0:2, :], in_=t_k0[:])
+            nc.scalar.copy(out=qkT[:, 2:4, :], in_=t_k1[:])
             live["qkT", 0] = qkT
 
         def vprep(u):
@@ -253,15 +250,9 @@ def tile_single_head_split_window_attention_1d_kernel(
         def rowmax(i):
             sp = stat.tile([P, WIN], F32, name="sp")
             negmax = stat.tile([P, 1], F32, name="negmax")
-            if i // 4 < ROWS:
-                src = live["s_ps", i][:]
-                dst = sp[:]
-            else:
-                src = live["s_ps", i][:].rearrange("q (u e x) -> q u x e", u=2, e=2)
-                dst = sp[:].rearrange("q (u x e) -> q u x e", u=2, e=2)
             nc.vector.tensor_scalar(
-                out=dst,
-                in0=src,
+                out=sp[:].rearrange("q (u x e) -> q u x e", u=2, e=2),
+                in0=live["s_ps", i][:].rearrange("q (u e x) -> q u x e", u=2, e=2),
                 scalar1=-scale,
                 scalar2=None,
                 op0=ALU.mult,
@@ -272,14 +263,16 @@ def tile_single_head_split_window_attention_1d_kernel(
 
         def biased(i):
             sp = stat.tile([P, WIN], F32, name="sp")
-            nc.vector.scalar_tensor_tensor(
-                out=sp[:],
-                in0=live["s_ps", i][:],
-                scalar=scale,
-                in1=b_sb[0][0][:, i, :],
-                op0=ALU.mult,
-                op1=ALU.add,
-            )
+            for u in range(2):
+                cols = slice(2 * P * u, 2 * P * u + 2 * P)
+                nc.vector.scalar_tensor_tensor(
+                    out=sp[:, cols].rearrange("q (x e) -> q x e", e=2),
+                    in0=live["s_ps", i][:, cols].rearrange("q (e x) -> q x e", e=2),
+                    scalar=scale,
+                    in1=b_sb[0][0][:, i, cols].rearrange("q (x e) -> q x e", e=2),
+                    op0=ALU.mult,
+                    op1=ALU.add,
+                )
             live["biased", i] = sp
 
         def biased_max(i):
@@ -410,18 +403,18 @@ def tile_single_head_split_window_attention_1d_kernel(
                 nc.sync.dma_start(out=o_v[:, g, :, :], in_=o_sb[:, 2 * b : 2 * b + 2, :])
 
         first_qk()
-        bias_t(0, 0, 1, ps_e, "eT")
-        bias_t(0, 1, 1, ps_e, "eT")
-        bias_ev(0, 0, 1, True)
-        bias_ev(0, 1, 1, False)
+        bias_t(0, 0, 2, ps_e, "eT")
+        bias_copy(0, 0, 2, False)
         qk(0, True)
         qk(1, True)
         bias_t(0, 2, 1, ps_o, "o_ps")
-        bias_ev(0, 2, 1, False)
+        bias_direct(0, 2)
         bias_t(0, 3, 1, ps_e, "eT")
-        bias_ev(0, 3, 1, False)
+        bias_direct(0, 3)
         tqk(1)
         evqk(1)
+        bias_spread(0, 0)
+        bias_spread(0, 1)
         biased(0)
         biased(1)
         biased_max(0)
@@ -432,14 +425,14 @@ def tile_single_head_split_window_attention_1d_kernel(
             if s <= UNITS:
                 vprep(s - 1)
             if 4 <= s <= 7:
-                bias_w_spread(s - 4)
+                bias_spread(1, s - 4)
             if m >= 1:
                 rowmax(2 * m)
                 if s >= 4 and s % 2 == 0:
                     recip((s - 4) // 2)
                 rowmax(2 * m + 1)
             if s in (2, 3):
-                bias_w_copy(2 * (s - 2))
+                bias_copy(1, 2 * (s - 2), 2, True)
             if s >= 4 and s % 2 == 0:
                 qnt((s - 4) // 2, 0, 4)
             if s in (3, 4, 6, 10):
@@ -455,7 +448,7 @@ def tile_single_head_split_window_attention_1d_kernel(
             if s % 2 == 0 and s // 2 + 1 < UNITS:
                 tqk(s // 2 + 1)
             if s in (1, 2):
-                bias_w(2 * (s - 1))
+                bias_t(1, 2 * (s - 1), 2, ps_o, "o_ps")
             if s >= 5 and s % 2 == 1 and s < PAIRS - 1:
                 outs((s - 5) // 2, 0, 4, True)
             if m % 2 == 0 and m // 2 + 1 < UNITS and s > 1:

@@ -110,12 +110,6 @@ def tile_single_head_split_window_attention_1d_kernel(
         warm2 = const.tile([P, 1], F32, name="warm2")
         nc.scalar.activation(out=warm2[:], in_=warm[:], func=ACT.Exp)
 
-        zeros = const.tile([P, WIN], BF16, name="zeros")
-        nc.vector.memset(zeros[:], 0.0)
-        for d in range(3):
-            z_ps = ps_s.tile([P, WIN], F32, name="z_ps", tag="s_ps")
-            nc.tensor.matmul(out=z_ps[:], lhsT=ident[:], rhs=zeros[:], start=True, stop=True)
-
         bp = [const.tile([P, 4, 4, P], F32, name="bp%d" % n) for n in range(NWIN)]
         v_groups = ((0, 1), (1, 1), (2, 2), (4, 4))
         v_q = {}

from contextlib import ExitStack

import concourse.mybir as mybir
from concourse.masks import make_identity

BF16 = mybir.dt.bfloat16
F32 = mybir.dt.float32
U32 = mybir.dt.uint32
U8 = mybir.dt.uint8
FP8X4 = mybir.dt.float8_e4m3fn_x4
ALU = mybir.AluOpType
ACT = mybir.ActivationFunctionType

P = 128
C = 128
ROWS = 4
WIN = 512
NWIN = 2
UNITS = ROWS * NWIN
PAIRS = 2 * UNITS
FLOPS = 2 * UNITS * 2 * WIN * WIN * C


def tile_single_head_split_window_attention_1d_kernel(
    tc, q, k, v, attn_mask, h, w, num_splits, out
):
    nc = tc.nc
    assert h == 2 and w == 1024 and num_splits == 2
    scale = 1.0 / (C ** 0.5)

    q_v = q.flatten_outer_dims().rearrange("(g p j) c -> p g j c", p=P, j=2)
    k_v = k.flatten_outer_dims().rearrange("(g p e) c -> p g e c", p=P, e=2)
    v_v = v.flatten_outer_dims().rearrange("(g p t) c -> g p t c", p=P // 2, t=4)
    b_v = attn_mask.rearrange("n (h p j) k -> p n h j k", p=P, j=2)
    o_v = out.flatten_outer_dims().rearrange("(g p j) c -> p g j c", p=P, j=2)

    with ExitStack() as ctx:
        const = ctx.enter_context(tc.tile_pool(name="const", bufs=1))
        work = ctx.enter_context(tc.tile_pool(name="work", bufs=4))
        stat = ctx.enter_context(tc.tile_pool(name="stat", bufs=8))
        ps_t = ctx.enter_context(tc.psum_pool(name="ps_t", bufs=1))
        ps_s = ctx.enter_context(tc.psum_pool(name="ps_s", bufs=4))
        ps_e = ctx.enter_context(tc.psum_pool(name="ps_e", bufs=2))
        ps_o = ctx.enter_context(tc.psum_pool(name="ps_o", bufs=1))
        ctx.enter_context(tc.manual_schedule())

        k_sb = [const.tile([P, 2, 2, C], BF16, name="k_sb%d" % u) for u in range(UNITS)]
        q_sb = [const.tile([P, 2, 2, C], BF16, name="q_sb%d" % u) for u in range(UNITS)]
        v_sb = [const.tile([P, 4, C], BF16, name="v_sb%d" % u) for u in range(UNITS)]
        b_sb = [
            [const.tile([P, 2, WIN], BF16, name="b_sb%d%d" % (n, hh)) for hh in range(2)]
            for n in range(NWIN)
        ]

        def load_k(u):
            r, n = u % ROWS, u // ROWS
            if n == 0:
                nc.sync.dma_start(out=k_sb[u][:], in_=k_v[:, 4 * r + 1 : 4 * r + 3, :, :])
            else:
                nc.sync.dma_start(out=k_sb[u][:, 0], in_=k_v[:, 4 * r + 3, :, :])
                nc.sync.dma_start(out=k_sb[u][:, 1], in_=k_v[:, 4 * r, :, :])

        def load_q(u):
            r, n = u % ROWS, u // ROWS
            if n == 0:
                nc.sync.dma_start(out=q_sb[u][:], in_=q_v[:, 4 * r + 1 : 4 * r + 3, :, :])
            else:
                nc.sync.dma_start(out=q_sb[u][:, 0], in_=q_v[:, 4 * r + 3, :, :])
                nc.sync.dma_start(out=q_sb[u][:, 1], in_=q_v[:, 4 * r, :, :])

        def load_v(u):
            r, n = u % ROWS, u // ROWS
            if n == 0:
                r0 = 4 * WIN // 2 * r + WIN // 2
                src = v.flatten_outer_dims()[r0 : r0 + WIN, :]
                nc.sync.dma_start(out=v_sb[u][:], in_=src.rearrange("(p t) c -> p t c", t=4))
            else:
                for hh in range(2):
                    nc.sync.dma_start(
                        out=v_sb[u][64 * hh : 64 * hh + 64],
                        in_=v_v[4 * r + (3 + hh) % 4],
                    )

        def load_bias(n):
            for hh in range(2):
                for j in range(2):
                    nc.sync.dma_start(out=b_sb[n][hh][:, j], in_=b_v[:, n, hh, j])

        for u in range(UNITS):
            if u == 0:
                load_q(u)
                load_k(u)
            else:
                load_k(u)
                load_q(u)
            if u == 0:
                load_bias(0)
            else:
                load_v(u - 1)
            if u == 1:
                load_bias(1)
        load_v(UNITS - 1)

        ident = const.tile([P, P], BF16, name="ident")
        make_identity(nc, ident[:])
        ident_f = const.tile([P, P], F32, name="ident_f")
        make_identity(nc, ident_f[:])
        warm = const.tile([P, 1], F32, name="warm")
        nc.vector.memset(warm[:], 0.0)
        warm2 = const.tile([P, 1], F32, name="warm2")
        nc.scalar.activation(out=warm2[:], in_=warm[:], func=ACT.Exp)

        bp = [const.tile([P, 4, 4, P], F32, name="bp%d" % n) for n in range(NWIN)]
        v_groups = ((0, 1), (1, 1), (2, 2), (4, 4))
        v_q = {}
        for u0, nu in v_groups:
            gv = const.tile([P, nu, C, 4], BF16, name="gv%d" % u0, align_bytes=64)
            codes = const.tile([P, nu, C], U32, name="v_codes%d" % u0, align_bytes=64)
            scales = const.tile([P, nu, C], U8, name="v_scales%d" % u0, align_bytes=64)
            for i in range(nu):
                v_q[u0 + i] = (gv, codes, scales, i)

        live = {}

        def bias_t(n, a0, na, pool, tag):
            bT = pool.tile([P, na, 2, P], F32, name="bT", tag=tag)
            for a in range(na):
                words = b_sb[n][(a0 + a) // 2][:, (a0 + a) % 2, :].bitcast(F32)
                for u in range(2):
                    nc.tensor.transpose(
                        out=bT[:, a, u, :],
                        in_=words[:, P * u : P * u + P],
                        identity=ident_f[:],
                    )
            live["bT", n, a0] = bT

        def bias_copy(n, a0, na, on_vector):
            bw = const.tile([P, na * 2 * P * 2], BF16, name="bw%d%d" % (n, a0))
            dst = bw[:].bitcast(F32)
            src = live["bT", n, a0][:].rearrange("p a u q -> p (a u q)")
            if on_vector:
                nc.vector.tensor_copy(out=dst, in_=src)
            else:
                nc.scalar.copy(out=dst, in_=src)
            for a in range(na):
                live["bw", n, a0 + a] = bw[:, 4 * P * a : 4 * P * a + 4 * P]

        def bias_spread(n, a):
            nc.gpsimd.tensor_scalar(
                out=bp[n][:, a, :, :].rearrange("p (u e) q -> p u e q", e=2),
                in0=live["bw", n, a].rearrange("p (u q e) -> p u e q", u=2, e=2),
                scalar1=C ** 0.5,
                scalar2=0.0,
                op0=ALU.mult,
                op1=ALU.add,
            )

        def bias_direct(n, a):
            pairs = live["bT", n, a][:].rearrange("p a u q -> p (a u q)").bitcast(BF16)
            nc.scalar.mul(
                out=bp[n][:, a, :, :].rearrange("p (u e) q -> p u e q", e=2),
                in_=pairs.rearrange("p (u q e) -> p u e q", u=2, e=2),
                mul=C ** 0.5,
            )

        def qk_source(u, i):
            src = k_sb[u] if i < 4 else q_sb[u]
            return src[:, i % 4 // 2, i % 2, :]

        def tqk(u):
            t_ps = ps_t.tile([P, 8, P], BF16, name="t_ps")
            for i in range(8):
                nc.tensor.transpose(out=t_ps[:, i, :], in_=qk_source(u, i), identity=ident[:])
            live["t_ps", u] = t_ps

        def evqk(u):
            qkT = work.tile([P, 8, P], BF16, name="qkT")
            nc.scalar.copy(
                out=qkT[:].rearrange("p i x -> p (i x)").bitcast(F32),
                in_=live["t_ps", u][:].rearrange("p i x -> p (i x)").bitcast(F32),
            )
            live["qkT", u] = qkT

        def first_qk():
            qkT = work.tile([P, 8, P], BF16, name="qkT")
            t_q = ps_s.tile([P, 4, P], BF16, name="t_q", tag="s_ps")
            t_k0 = ps_t.tile([P, 2, P], BF16, name="t_k0", tag="t_ps")
            t_k1 = ps_o.tile([P, 2, P], BF16, name="t_k1", tag="o_ps")
            for i in range(4):
                nc.tensor.transpose(out=t_q[:, i, :], in_=qk_source(0, 4 + i), identity=ident[:])
            for i in range(2):
                nc.tensor.transpose(out=t_k0[:, i, :], in_=qk_source(0, i), identity=ident[:])
            for i in range(2):
                nc.tensor.transpose(out=t_k1[:, i, :], in_=qk_source(0, 2 + i), identity=ident[:])
            nc.scalar.copy(out=qkT[:, 4:8, :], in_=t_q[:])
            nc.vector.tensor_copy(out=qkT[:, 0:2, :], in_=t_k0[:])
            nc.scalar.copy(out=qkT[:, 2:4, :], in_=t_k1[:])
            live["qkT", 0] = qkT

        def vprep(u):
            gv, codes, scales, i = v_q[u]
            nc.gpsimd.tensor_scalar(
                out=gv[:, i],
                in0=v_sb[u][:].rearrange("p t c -> p c t"),
                scalar1=1.0,
                scalar2=0.0,
                op0=ALU.mult,
                op1=ALU.add,
            )

        def vquant(u0):
            gv, codes, scales, i = v_q[u0]
            nc.vector.quantize_mx(
                out=codes[:].rearrange("p u c -> p (u c)").bitcast(FP8X4),
                scales=scales[:].rearrange("p u c -> p (u c)"),
                in_=gv[:].rearrange("p u c t -> p (u c t)"),
            )

        def qk(i, alone=False):
            u, a = i // 4, i % 4
            qkT = live["qkT", u]
            s_ps = ps_s.tile([P, WIN], F32, name="s_ps")
            nc.tensor.matmul(
                out=s_ps[:],
                lhsT=qkT[:, 4 + a, :],
                rhs=qkT[:, 0:4, :].rearrange("p t k -> p (t k)"),
                start=True,
                stop=alone,
            )
            live["s_ps", i] = s_ps

        def addbias(i):
            u, a = i // 4, i % 4
            for t in range(4):
                nc.tensor.matmul(
                    out=live["s_ps", i][:, P * t : P * t + P],
                    lhsT=bp[u // ROWS][:, a, t, :],
                    rhs=ident_f[:],
                    is_transpose=True,
                    start=False,
                    stop=(t == 3),
                )

        def rowmax(i):
            sp = stat.tile([P, WIN], F32, name="sp")
            negmax = stat.tile([P, 1], F32, name="negmax")
            nc.vector.tensor_scalar(
                out=sp[:].rearrange("q (u x e) -> q u x e", u=2, e=2),
                in0=live["s_ps", i][:].rearrange("q (u e x) -> q u x e", u=2, e=2),
                scalar1=-scale,
                scalar2=None,
                op0=ALU.mult,
                op1=ALU.min,
                accum_out=negmax[:],
            )
            live["sp", i] = (sp, negmax, -1.0)

        def biased(i):
            sp = stat.tile([P, WIN], F32, name="sp")
            for u in range(2):
                cols = slice(2 * P * u, 2 * P * u + 2 * P)
                nc.vector.scalar_tensor_tensor(
                    out=sp[:, cols].rearrange("q (x e) -> q x e", e=2),
                    in0=live["s_ps", i][:, cols].rearrange("q (e x) -> q x e", e=2),
                    scalar=scale,
                    in1=b_sb[0][0][:, i, cols].rearrange("q (x e) -> q x e", e=2),
                    op0=ALU.mult,
                    op1=ALU.add,
                )
            live["biased", i] = sp

        def biased_max(i):
            sp = live["biased", i]
            negmax = stat.tile([P, 1], F32, name="negmax")
            nc.vector.reduce_max(out=negmax[:], in_=sp[:], axis=mybir.AxisListType.X, negate=True)
            live["sp", i] = (sp, negmax, 1.0)

        def expo(i):
            u, a = i // 4, i % 4
            if a == 0:
                live["rowsum", u] = stat.tile([P, 4], F32, name="rowsum")
            if a % 2 == 0:
                live["e", i // 2] = work.tile([P, 2, WIN], BF16, name="e_sb")
            sp, negmax, sign = live["sp", i]
            nc.scalar.activation(
                out=live["e", i // 2][:, a % 2, :].rearrange("q (u p e) -> q u p e", u=2, e=2),
                in_=sp[:].rearrange("q (p u e) -> q u p e", u=2, e=2),
                func=ACT.Exp,
                bias=negmax[:],
                scale=sign,
                accum_out=live["rowsum", u][:, a : a + 1],
            )

        def te(j):
            eT = ps_e.tile([P, 2, 2, P], F32, name="eT")
            words = live["e", j][:].rearrange("q a k -> q (a k)").bitcast(F32)
            for a in range(2):
                for u in range(2):
                    nc.tensor.transpose(
                        out=eT[:, a, u, :],
                        in_=words[:, 2 * P * a + P * u : 2 * P * a + P * u + P],
                        identity=ident_f[:],
                    )
            live["eT", j] = eT

        def g_words(i, na):
            u, a = i // 4, i % 4
            if a == 0:
                live["g", u] = work.tile([P, 4 * P * 4], BF16, name="g_sb", align_bytes=64)
            words = live["g", u][:].bitcast(F32)[:, 2 * P * a : 2 * P * (a + na)]
            return words.rearrange("p (a q u) -> p a q u", a=na, u=2)

        def eve(j, on_vector):
            dst = g_words(2 * j, 2)
            src = live["eT", j][:].rearrange("p a u q -> p a q u")
            if on_vector:
                nc.vector.tensor_copy(out=dst, in_=src)
            else:
                nc.scalar.copy(out=dst, in_=src)

        def te_one(i):
            eT1 = ps_s.tile([P, 2, P], F32, name="eT1", tag="s_ps")
            words = live["e", i // 2][:].rearrange("q a k -> q (a k)").bitcast(F32)
            for u in range(2):
                w0 = 2 * P * (i % 2) + P * u
                nc.tensor.transpose(
                    out=eT1[:, u, :], in_=words[:, w0 : w0 + P], identity=ident_f[:]
                )
            live["eT1", i] = eT1

        def eve_one(i, on_vector):
            dst = g_words(i, 1)
            src = live["eT1", i][:].rearrange("p u q -> p q u").unsqueeze(1)
            if on_vector:
                nc.vector.tensor_copy(out=dst, in_=src)
            else:
                nc.scalar.copy(out=dst, in_=src)

        def qnt(u, a0, na):
            if a0 == 0:
                live["c", u] = (
                    work.tile([P, 4 * P], U32, name="e_codes", align_bytes=64),
                    work.tile([P, 4 * P], U8, name="e_scales", align_bytes=64),
                )
            e_codes, e_scales = live["c", u]
            nc.vector.quantize_mx(
                out=e_codes[:, P * a0 : P * (a0 + na)].bitcast(FP8X4),
                scales=e_scales[:, P * a0 : P * (a0 + na)],
                in_=live["g", u][:, 4 * P * a0 : 4 * P * (a0 + na)],
            )

        def mx(u, a0, na, pool, tag):
            e_codes, e_scales = live["c", u]
            gv, v_codes, v_scales, i = v_q[u]
            o_ps = pool.tile([P, na, C], F32, name="o_ps", tag=tag)
            for a in range(na):
                c0 = P * (a0 + a)
                nc.tensor.matmul_mx(
                    out=o_ps[:, a, :],
                    lhsT=e_codes[:, c0 : c0 + P].bitcast(FP8X4),
                    lhsT_scale=e_scales[:, c0 : c0 + P],
                    rhs=v_codes[:, i, :].bitcast(FP8X4),
                    rhs_scale=v_scales[:, i, :],
                    start=True,
                    stop=True,
                )
            live["o", u, a0] = o_ps

        def recip(u):
            rinv = stat.tile([P, 4], F32, name="rinv")
            nc.vector.reciprocal(out=rinv[:], in_=live["rowsum", u][:])
            live["rinv", u] = rinv

        def outs(u, a0, na, on_vector):
            r, n = u % ROWS, u // ROWS
            rinv = live["rinv", u]
            o_ps = live["o", u, a0]
            o_sb = work.tile([P, na, C], F32, name="o_sb")
            if on_vector:
                nc.vector.tensor_tensor(
                    out=o_sb[:],
                    in0=o_ps[:],
                    in1=rinv[:, a0 : a0 + na].unsqueeze(2).to_broadcast([P, na, C]),
                    op=ALU.mult,
                )
            else:
                for a in range(na):
                    nc.scalar.activation(
                        out=o_sb[:, a, :],
                        in_=o_ps[:, a, :],
                        func=ACT.Copy,
                        scale=rinv[:, a0 + a : a0 + a + 1],
                    )
            for b in range(na // 2):
                hh = a0 // 2 + b
                g = 4 * r + (1 + 2 * n + hh) % 4
                nc.sync.dma_start(out=o_v[:, g, :, :], in_=o_sb[:, 2 * b : 2 * b + 2, :])

        first_qk()
        bias_t(0, 0, 2, ps_e, "eT")
        bias_copy(0, 0, 2, False)
        qk(0, True)
        qk(1, True)
        bias_t(0, 2, 1, ps_o, "o_ps")
        bias_direct(0, 2)
        bias_t(0, 3, 1, ps_e, "eT")
        bias_direct(0, 3)
        tqk(1)
        evqk(1)
        bias_spread(0, 0)
        bias_spread(0, 1)
        biased(0)
        biased(1)
        biased_max(0)
        biased_max(1)

        for s in range(1, PAIRS):
            m = s - 1
            if s <= UNITS:
                vprep(s - 1)
            if 4 <= s <= 7:
                bias_spread(1, s - 4)
            if m >= 1:
                rowmax(2 * m)
                if s >= 4 and s % 2 == 0:
                    recip((s - 4) // 2)
                rowmax(2 * m + 1)
            if s in (2, 3):
                bias_copy(1, 2 * (s - 2), 2, True)
            if s >= 4 and s % 2 == 0:
                qnt((s - 4) // 2, 0, 4)
            if s in (3, 4, 6, 10):
                vquant({3: 0, 4: 1, 6: 2, 10: 4}[s])
            qk(2 * s)
            if s >= 5 and s % 2 == 1 and s < PAIRS - 1:
                mx((s - 5) // 2, 0, 4, ps_o, "o_ps")
            qk(2 * s + 1)
            addbias(2 * s)
            addbias(2 * s + 1)
            if s >= 2:
                te(s - 2)
            if s % 2 == 0 and s // 2 + 1 < UNITS:
                tqk(s // 2 + 1)
            if s in (1, 2):
                bias_t(1, 2 * (s - 1), 2, ps_o, "o_ps")
            if s >= 5 and s % 2 == 1 and s < PAIRS - 1:
                outs((s - 5) // 2, 0, 4, True)
            if m % 2 == 0 and m // 2 + 1 < UNITS and s > 1:
                evqk(m // 2 + 1)
            expo(2 * m)
            expo(2 * m + 1)
            if m >= 1:
                eve(m - 1, False)

        mx(5, 0, 4, ps_o, "o_ps")
        te(14)
        rowmax(30)
        rowmax(31)
        expo(30)
        expo(31)
        te_one(30)
        te_one(31)
        recip(6)
        outs(5, 0, 4, True)
        qnt(6, 0, 4)
        mx(6, 0, 4, ps_o, "o_ps")
        eve(14, True)
        recip(7)
        eve_one(30, True)
        eve_one(31, False)
        qnt(7, 0, 2)
        mx(7, 0, 2, ps_s, "s_ps")
        qnt(7, 2, 2)
        mx(7, 2, 2, ps_s, "s_ps")
        outs(6, 0, 4, False)
        outs(7, 0, 2, True)
        outs(7, 2, 2, True)
